import numpy as np
import ml_dtypes


def mxq(x, axis, fmt="e4m3"):
    dtype, down = {"e4m3": (ml_dtypes.float8_e4m3fn, 7), "e5m2": (ml_dtypes.float8_e5m2, 14)}[fmt]
    v = np.moveaxis(np.asarray(x, np.float32).astype(ml_dtypes.bfloat16).astype(np.float64), axis, -1)
    blocks = v.reshape(v.shape[:-1] + (-1, 32))
    amax = np.abs(blocks).max(-1, keepdims=True)
    byte = np.maximum(np.where(amax > 0, np.frexp(amax)[1] - 1 + 127, 0) - down, 1)
    scale = np.exp2(byte - 127.0)
    codes = (blocks / scale).astype(np.float32).astype(dtype).astype(np.float64)
    return np.moveaxis((codes * scale).reshape(v.shape), -1, axis)


BF16 = ml_dtypes.bfloat16


def bf(x):
    return np.asarray(x, np.float32).astype(BF16)


def f64(x):
    return np.asarray(x).astype(np.float64)


N, CK, CV, T, H, W = 2, 128, 256, 4, 16, 16
Q = H * W
M = T * Q


def setup_inputs():
    return {"q_key": bf(np.random.standard_normal((N, CK, H, W))),
            "q_val": bf(np.random.standard_normal((N, CV, H, W))),
            "m_key": bf(np.random.standard_normal((N, CK, T, H, W))),
            "m_val": bf(np.random.standard_normal((N, CV, T, H, W)) * 0.5 * Q / np.sqrt(M))}


def reference(q_key, q_val, m_key, m_val):
    qk = f64(q_key).reshape(N, CK, Q)
    mk = f64(m_key).reshape(N, CK, M)
    aff = (qk.transpose(0, 2, 1) @ mk) * (CK ** -0.5)
    e = np.exp(aff - aff.max(axis=1, keepdims=True))
    attn = e / e.sum(axis=1, keepdims=True)
    mv = f64(m_val).reshape(N, CV, M)
    mapped = (mxq(mv, 2, "e4m3") @ mxq(attn, 2, "e4m3").transpose(0, 2, 1)).reshape(N, CV, H, W)
    return np.concatenate([f64(q_val), mapped], axis=1)

@@ -1,0 +1,195 @@
+import math
+
+import concourse.mybir as mybir
+from concourse.masks import make_identity
+
+F32 = mybir.dt.float32
+BF16 = mybir.dt.bfloat16
+U32 = mybir.dt.uint32
+U8 = mybir.dt.uint8
+FP8X4 = mybir.dt.float8_e4m3fn_x4
+
+P = 128
+SAMPLES = 2
+CK = 128
+CV = 256
+Q = 256
+M = 1024
+PACK = 4
+K_PASS = P * PACK
+PASSES = M // K_PASS
+GROUPS = SAMPLES * PASSES
+HALVES = 2
+PAIR = 2
+C_TILES = CV // P
+SCALE = 1.0 / math.sqrt(CK)
+
+FLOPS = 2 * SAMPLES * Q * M * (CK + CV)
+
+
+def tile_stm_head_s_kernel(tc, q_key, q_val, m_key, m_val, out):
+    nc = tc.nc
+    with (
+        tc.tile_pool(name="keep", bufs=1) as keep,
+        tc.tile_pool(name="work", bufs=GROUPS) as work,
+        tc.psum_pool(name="aff_psum", bufs=6) as aff_psum,
+        tc.psum_pool(name="aux_psum", bufs=2) as aux_psum,
+    ):
+        qk_sb = keep.tile([P, SAMPLES, Q], BF16)
+        mk_sb = keep.tile([P, SAMPLES, M], BF16)
+        mv_sb = keep.tile([P, SAMPLES, C_TILES, M], BF16)
+        qv_sb = keep.tile([P, SAMPLES, C_TILES, Q], BF16)
+        for n in range(SAMPLES):
+            nc.sync.dma_start(out=qk_sb[:, n, :], in_=q_key[n].rearrange("c h w -> c (h w)"))
+            nc.sync.dma_start(out=mk_sb[:, n, :], in_=m_key[n].rearrange("c t h w -> c (t h w)"))
+        for n in range(SAMPLES):
+            nc.sync.dma_start(out=mv_sb[:, n], in_=m_val[n].rearrange("(j r) t h w -> r j (t h w)", r=P))
+        for n in range(SAMPLES):
+            nc.sync.dma_start(out=qv_sb[:, n], in_=q_val[n].rearrange("(j r) h w -> r j (h w)", r=P))
+
+        ident = keep.tile([P, P], F32)
+        make_identity(nc, ident[:])
+        warm = keep.tile([P, 1], F32)
+        nc.vector.memset(warm[:], 0.0)
+        nc.scalar.activation(out=warm[:], in_=warm[:], func=mybir.ActivationFunctionType.Exp)
+
+        attn_codes = keep.tile([P, GROUPS, Q], U32, align_bytes=64)
+        attn_scales = keep.tile([P, GROUPS, Q], U8, align_bytes=64)
+        mv_codes = keep.tile([P, GROUPS, CV], U32, align_bytes=64)
+        mv_scales = keep.tile([P, GROUPS, CV], U8, align_bytes=64)
+
+        aff_banks = {}
+        exps = {}
+        attn_grouped = {}
+        mv_grouped = {}
+        sums = {}
+
+        def affinity(i):
+            n, g = divmod(i, PASSES)
+            keys = mk_sb[:, n, :].rearrange("c (g u p e) -> c g u e p", g=PASSES, u=HALVES, e=PAIR)
+            for u in range(HALVES):
+                bank = aff_psum.tile([P, PAIR, Q], F32)
+                for e in range(PAIR):
+                    nc.tensor.matmul(
+                        out=bank[:, e, :],
+                        lhsT=keys[:, g, u, e, :],
+                        rhs=qk_sb[:, n, :],
+                        start=True,
+                        stop=True,
+                    )
+                aff_banks[i, u] = bank
+
+        def exponentials(i):
+            top = work.tile([P, PACK], F32)
+            for u in range(HALVES):
+                nc.vector.tensor_reduce(
+                    out=top[:, PAIR * u : PAIR * (u + 1)],
+                    in_=aff_banks[i, u][:],
+                    axis=mybir.AxisListType.X,
+                    op=mybir.AluOpType.max,
+                )
+            shift = work.tile([P, PACK], F32)
+            nc.vector.tensor_scalar_mul(out=shift[:], in0=top[:], scalar1=-SCALE)
+            expd = work.tile([P, PACK, Q], F32)
+            total = work.tile([P, PACK], F32)
+            for u in range(HALVES):
+                for e in range(PAIR):
+                    t = PAIR * u + e
+                    nc.scalar.activation(
+                        out=expd[:, t, :],
+                        in_=aff_banks[i, u][:, e, :],
+                        func=mybir.ActivationFunctionType.Exp,
+                        bias=shift[:, t : t + 1],
+                        scale=SCALE,
+                        accum_out=total[:, t : t + 1],
+                    )
+            exps[i] = (expd, total)
+
+        def normalise(i):
+            expd, total = exps[i]
+            inverse = work.tile([P, PACK], F32)
+            nc.vector.reciprocal(out=inverse[:], in_=total[:])
+            grouped = work.tile([P, Q, PACK], BF16, align_bytes=64)
+            nc.vector.tensor_tensor(
+                out=grouped[:],
+                in0=expd[:].rearrange("p t q -> p q t"),
+                in1=inverse[:].unsqueeze(1).to_broadcast([P, Q, PACK]),
+                op=mybir.AluOpType.mult,
+            )
+            attn_grouped[i] = grouped
+
+        def transpose_values(n):
+            turned = work.tile([P, PASSES, CV, PACK], BF16, align_bytes=64)
+            for g in range(PASSES):
+                landing = aux_psum.tile([P, HALVES, C_TILES, P], F32, tag="aux")
+                for u in range(HALVES):
+                    for j in range(C_TILES):
+                        words = mv_sb[:, n, j, :].bitcast(F32)
+                        first = (K_PASS * g + PAIR * P * u) // PAIR
+                        nc.tensor.transpose(landing[:, u, j, :], words[:, first : first + P], ident[:])
+                nc.scalar.copy(
+                    out=turned[:, g].rearrange("p c t -> p (c t)").bitcast(F32).rearrange("p (c u) -> p c u", u=HALVES),
+                    in_=landing[:].rearrange("p u j r -> p (j r) u"),
+                )
+            mv_grouped[n] = turned
+
+        def quantise_values(n):
+            both = slice(PASSES * n, PASSES * (n + 1))
+            nc.vector.quantize_mx(
+                out=mv_codes[:, both, :].rearrange("p g c -> p (g c)").bitcast(FP8X4),
+                scales=mv_scales[:, both, :].rearrange("p g c -> p (g c)"),
+                in_=mv_grouped[n][:].rearrange("p g c t -> p (g c t)"),
+            )
+
+        def quantise_attn(i):
+            nc.vector.quantize_mx(
+                out=attn_codes[:, i, :].bitcast(FP8X4),
+                scales=attn_scales[:, i, :],
+                in_=attn_grouped[i][:].rearrange("p q t -> p (q t)"),
+            )
+
+        def read_out(i):
+            n, g = divmod(i, PASSES)
+            for j in range(C_TILES):
+                if g == 0:
+                    sums[n, j] = aux_psum.tile([P, Q], F32, tag="aux", name="mapped_sum")
+                channels = slice(P * j, P * (j + 1))
+                nc.tensor.matmul_mx(
+                    out=sums[n, j][:],
+                    lhsT=mv_codes[:, i, channels].bitcast(FP8X4),
+                    lhsT_scale=mv_scales[:, i, channels],
+                    rhs=attn_codes[:, i, :].bitcast(FP8X4),
+                    rhs_scale=attn_scales[:, i, :],
+                    start=(g == 0),
+                    stop=(g == PASSES - 1),
+                )
+            if g == PASSES - 1:
+                for j in range(C_TILES):
+                    mapped = work.tile([P, Q], F32)
+                    nc.scalar.copy(out=mapped[:], in_=sums[n, j][:])
+                    rows = slice(CV + P * j, CV + P * (j + 1))
+                    nc.sync.dma_start(out=out[n, rows].rearrange("r h w -> r (h w)"), in_=mapped[:])
+
+        def pass_query_values():
+            for n in range(SAMPLES):
+                wide = work.tile([P, C_TILES, Q], F32)
+                nc.scalar.copy(out=wide[:], in_=qv_sb[:, n])
+                nc.sync.dma_start(out=out[n, 0:CV].rearrange("(j r) h w -> r j (h w)", r=P), in_=wide[:])
+
+        affinity(0)
+        for i in range(GROUPS + 3):
+            if i + 1 < GROUPS:
+                affinity(i + 1)
+            if i < GROUPS:
+                exponentials(i)
+            if 1 <= i <= SAMPLES:
+                transpose_values(i - 1)
+            if i == GROUPS:
+                pass_query_values()
+            if 0 <= i - 2 < GROUPS:
+                normalise(i - 2)
+            if 0 <= i - 3 < GROUPS:
+                if i - 3 < SAMPLES:
+                    quantise_values(i - 3)
+                quantise_attn(i - 3)
+                read_out(i - 3)

@@ -176,20 +176,21 @@ def tile_stm_head_s_kernel(tc, q_key, q_val, m_key, m_val, out):
                 nc.scalar.copy(out=wide[:], in_=qv_sb[:, n])
                 nc.sync.dma_start(out=out[n, 0:CV].rearrange("(j r) h w -> r j (h w)", r=P), in_=wide[:])
 
-        affinity(0)
-        for i in range(GROUPS + 3):
-            if i + 1 < GROUPS:
-                affinity(i + 1)
-            if i < GROUPS:
-                exponentials(i)
-            if 1 <= i <= SAMPLES:
-                transpose_values(i - 1)
-            if i == GROUPS:
-                pass_query_values()
-            if 0 <= i - 2 < GROUPS:
-                normalise(i - 2)
-            if 0 <= i - 3 < GROUPS:
-                if i - 3 < SAMPLES:
-                    quantise_values(i - 3)
-                quantise_attn(i - 3)
-                read_out(i - 3)
+        with tc.manual_schedule():
+            affinity(0)
+            for i in range(GROUPS + 3):
+                if i + 1 < GROUPS:
+                    affinity(i + 1)
+                if i < GROUPS:
+                    exponentials(i)
+                if 1 <= i <= SAMPLES:
+                    transpose_values(i - 1)
+                if i == GROUPS:
+                    pass_query_values()
+                if 0 <= i - 2 < GROUPS:
+                    normalise(i - 2)
+                if 0 <= i - 3 < GROUPS:
+                    if i - 3 < SAMPLES:
+                        quantise_values(i - 3)
+                    quantise_attn(i - 3)
+                    read_out(i - 3)

@@ -32,8 +32,7 @@ def tile_stm_head_s_kernel(tc, q_key, q_val, m_key, m_val, out):
     with (
         tc.tile_pool(name="keep", bufs=1) as keep,
         tc.tile_pool(name="work", bufs=GROUPS) as work,
-        tc.psum_pool(name="aff_psum", bufs=6) as aff_psum,
-        tc.psum_pool(name="aux_psum", bufs=2) as aux_psum,
+        tc.psum_pool(name="psum", bufs=8) as psum,
     ):
         qk_sb = keep.tile([P, SAMPLES, Q], BF16)
         mk_sb = keep.tile([P, SAMPLES, M], BF16)
@@ -42,10 +41,9 @@ def tile_stm_head_s_kernel(tc, q_key, q_val, m_key, m_val, out):
         for n in range(SAMPLES):
             nc.sync.dma_start(out=qk_sb[:, n, :], in_=q_key[n].rearrange("c h w -> c (h w)"))
             nc.sync.dma_start(out=mk_sb[:, n, :], in_=m_key[n].rearrange("c t h w -> c (t h w)"))
+            nc.sync.dma_start(out=qv_sb[:, n], in_=q_val[n].rearrange("(j r) h w -> r j (h w)", r=P))
         for n in range(SAMPLES):
             nc.sync.dma_start(out=mv_sb[:, n], in_=m_val[n].rearrange("(j r) t h w -> r j (t h w)", r=P))
-        for n in range(SAMPLES):
-            nc.sync.dma_start(out=qv_sb[:, n], in_=q_val[n].rearrange("(j r) h w -> r j (h w)", r=P))
 
         ident = keep.tile([P, P], F32)
         make_identity(nc, ident[:])
@@ -68,7 +66,7 @@ def tile_stm_head_s_kernel(tc, q_key, q_val, m_key, m_val, out):
             n, g = divmod(i, PASSES)
             keys = mk_sb[:, n, :].rearrange("c (g u p e) -> c g u e p", g=PASSES, u=HALVES, e=PAIR)
             for u in range(HALVES):
-                bank = aff_psum.tile([P, PAIR, Q], F32)
+                bank = psum.tile([P, PAIR, Q], F32, tag="bank")
                 for e in range(PAIR):
                     nc.tensor.matmul(
                         out=bank[:, e, :],
@@ -80,37 +78,34 @@ def tile_stm_head_s_kernel(tc, q_key, q_val, m_key, m_val, out):
                 aff_banks[i, u] = bank
 
         def exponentials(i):
-            top = work.tile([P, PACK], F32)
-            for u in range(HALVES):
-                nc.vector.tensor_reduce(
-                    out=top[:, PAIR * u : PAIR * (u + 1)],
-                    in_=aff_banks[i, u][:],
-                    axis=mybir.AxisListType.X,
-                    op=mybir.AluOpType.max,
-                )
-            shift = work.tile([P, PACK], F32)
-            nc.vector.tensor_scalar_mul(out=shift[:], in0=top[:], scalar1=-SCALE)
             expd = work.tile([P, PACK, Q], F32)
             total = work.tile([P, PACK], F32)
             for u in range(HALVES):
+                top = work.tile([P, PAIR], F32, bufs=HALVES * GROUPS)
+                nc.vector.tensor_reduce(
+                    out=top[:], in_=aff_banks[i, u][:], axis=mybir.AxisListType.X, op=mybir.AluOpType.max
+                )
+                shift = work.tile([P, PAIR], F32, bufs=HALVES * GROUPS)
+                nc.scalar.mul(out=shift[:], in_=top[:], mul=-SCALE)
                 for e in range(PAIR):
                     t = PAIR * u + e
                     nc.scalar.activation(
                         out=expd[:, t, :],
                         in_=aff_banks[i, u][:, e, :],
                         func=mybir.ActivationFunctionType.Exp,
-                        bias=shift[:, t : t + 1],
+                        bias=shift[:, e : e + 1],
                         scale=SCALE,
                         accum_out=total[:, t : t + 1],
                     )
-            exps[i] = (expd, total)
-
-        def normalise(i):
-            expd, total = exps[i]
             inverse = work.tile([P, PACK], F32)
             nc.vector.reciprocal(out=inverse[:], in_=total[:])
+            exps[i] = (expd, inverse)
+
+        def normalise(i):
+            expd, inverse = exps[i]
             grouped = work.tile([P, Q, PACK], BF16, align_bytes=64)
-            nc.vector.tensor_tensor(
+            engine = nc.gpsimd if i == 0 else nc.vector
+            engine.tensor_tensor(
                 out=grouped[:],
                 in0=expd[:].rearrange("p t q -> p q t"),
                 in1=inverse[:].unsqueeze(1).to_broadcast([P, Q, PACK]),
@@ -121,7 +116,7 @@ def tile_stm_head_s_kernel(tc, q_key, q_val, m_key, m_val, out):
         def transpose_values(n):
             turned = work.tile([P, PASSES, CV, PACK], BF16, align_bytes=64)
             for g in range(PASSES):
-                landing = aux_psum.tile([P, HALVES, C_TILES, P], F32, tag="aux")
+                landing = psum.tile([P, HALVES, C_TILES, P], F32, tag="bank")
                 for u in range(HALVES):
                     for j in range(C_TILES):
                         words = mv_sb[:, n, j, :].bitcast(F32)
@@ -152,7 +147,7 @@ def tile_stm_head_s_kernel(tc, q_key, q_val, m_key, m_val, out):
             n, g = divmod(i, PASSES)
             for j in range(C_TILES):
                 if g == 0:
-                    sums[n, j] = aux_psum.tile([P, Q], F32, tag="aux", name="mapped_sum")
+                    sums[n, j] = psum.tile([P, Q], F32, tag="bank", name="mapped_sum")
                 channels = slice(P * j, P * (j + 1))
                 nc.tensor.matmul_mx(
                     out=sums[n, j][:],
@@ -173,24 +168,28 @@ def tile_stm_head_s_kernel(tc, q_key, q_val, m_key, m_val, out):
         def pass_query_values():
             for n in range(SAMPLES):
                 wide = work.tile([P, C_TILES, Q], F32)
-                nc.scalar.copy(out=wide[:], in_=qv_sb[:, n])
+                nc.gpsimd.tensor_scalar(
+                    out=wide[:],
+                    in0=qv_sb[:, n],
+                    scalar1=1.0,
+                    scalar2=0.0,
+                    op0=mybir.AluOpType.mult,
+                    op1=mybir.AluOpType.add,
+                )
                 nc.sync.dma_start(out=out[n, 0:CV].rearrange("(j r) h w -> r j (h w)", r=P), in_=wide[:])
 
-        with tc.manual_schedule():
-            affinity(0)
-            for i in range(GROUPS + 3):
-                if i + 1 < GROUPS:
-                    affinity(i + 1)
-                if i < GROUPS:
-                    exponentials(i)
-                if 1 <= i <= SAMPLES:
-                    transpose_values(i - 1)
-                if i == GROUPS:
-                    pass_query_values()
-                if 0 <= i - 2 < GROUPS:
-                    normalise(i - 2)
-                if 0 <= i - 3 < GROUPS:
-                    if i - 3 < SAMPLES:
-                        quantise_values(i - 3)
-                    quantise_attn(i - 3)
-                    read_out(i - 3)
+        for i in range(GROUPS):
+            affinity(i)
+        pass_query_values()
+        for i in range(GROUPS + 3):
+            if i < GROUPS:
+                exponentials(i)
+            if 1 <= i <= SAMPLES:
+                transpose_values(i - 1)
+            if 0 <= i - 2 < GROUPS:
+                normalise(i - 2)
+            if 0 <= i - 3 < GROUPS:
+                if i - 3 < SAMPLES:
+                    quantise_values(i - 3)
+                quantise_attn(i - 3)
+                read_out(i - 3)

@@ -38,10 +38,21 @@ def tile_stm_head_s_kernel(tc, q_key, q_val, m_key, m_val, out):
         mk_sb = keep.tile([P, SAMPLES, M], BF16)
         mv_sb = keep.tile([P, SAMPLES, C_TILES, M], BF16)
         qv_sb = keep.tile([P, SAMPLES, C_TILES, Q], BF16)
-        for n in range(SAMPLES):
+
+        def load_queries(n):
             nc.sync.dma_start(out=qk_sb[:, n, :], in_=q_key[n].rearrange("c h w -> c (h w)"))
-            nc.sync.dma_start(out=mk_sb[:, n, :], in_=m_key[n].rearrange("c t h w -> c (t h w)"))
-            nc.sync.dma_start(out=qv_sb[:, n], in_=q_val[n].rearrange("(j r) h w -> r j (h w)", r=P))
+
+        def load_keys(n, columns):
+            nc.sync.dma_start(out=mk_sb[:, n, columns], in_=m_key[n].rearrange("c t h w -> c (t h w)")[:, columns])
+
+        load_queries(0)
+        load_keys(0, slice(0, K_PASS))
+        load_keys(0, slice(K_PASS, M))
+        nc.sync.dma_start(
+            out=qv_sb[:].rearrange("r n j q -> r (n j) q"), in_=q_val.rearrange("n (j r) h w -> r (n j) (h w)", r=P)
+        )
+        load_queries(1)
+        load_keys(1, slice(0, M))
         for n in range(SAMPLES):
             nc.sync.dma_start(out=mv_sb[:, n], in_=m_val[n].rearrange("(j r) t h w -> r j (t h w)", r=P))
 
@@ -55,141 +66,195 @@ def tile_stm_head_s_kernel(tc, q_key, q_val, m_key, m_val, out):
         attn_scales = keep.tile([P, GROUPS, Q], U8, align_bytes=64)
         mv_codes = keep.tile([P, GROUPS, CV], U32, align_bytes=64)
         mv_scales = keep.tile([P, GROUPS, CV], U8, align_bytes=64)
+        attn_grouped = keep.tile([P, GROUPS, Q, PACK], BF16, align_bytes=64)
+        mv_grouped = keep.tile([P, GROUPS, CV, PACK], BF16, align_bytes=64)
 
         aff_banks = {}
+        aff_tiles = {}
+        tops = {}
+        shifts = {}
         exps = {}
-        attn_grouped = {}
-        mv_grouped = {}
+        landings = {}
         sums = {}
 
-        def affinity(i):
-            n, g = divmod(i, PASSES)
+        def affinity(b):
+            n, g, u = b // (PASSES * HALVES), b // HALVES % PASSES, b % HALVES
             keys = mk_sb[:, n, :].rearrange("c (g u p e) -> c g u e p", g=PASSES, u=HALVES, e=PAIR)
-            for u in range(HALVES):
+            if b == 0:
+                tiles = [psum.tile([P, 1, Q], F32, tag="bank", name="first_bank")[:] for e in range(PAIR)]
+            else:
                 bank = psum.tile([P, PAIR, Q], F32, tag="bank")
-                for e in range(PAIR):
-                    nc.tensor.matmul(
-                        out=bank[:, e, :],
-                        lhsT=keys[:, g, u, e, :],
-                        rhs=qk_sb[:, n, :],
-                        start=True,
-                        stop=True,
-                    )
-                aff_banks[i, u] = bank
-
-        def exponentials(i):
-            expd = work.tile([P, PACK, Q], F32)
-            total = work.tile([P, PACK], F32)
-            for u in range(HALVES):
-                top = work.tile([P, PAIR], F32, bufs=HALVES * GROUPS)
-                nc.vector.tensor_reduce(
-                    out=top[:], in_=aff_banks[i, u][:], axis=mybir.AxisListType.X, op=mybir.AluOpType.max
+                tiles = [bank[:, e : e + 1, :] for e in range(PAIR)]
+                aff_banks[b] = bank
+            for e in range(PAIR):
+                aff_tiles[b, e] = tiles[e]
+                nc.tensor.matmul(
+                    out=tiles[e].rearrange("p e q -> p (e q)"),
+                    lhsT=keys[:, g, u, e, :],
+                    rhs=qk_sb[:, n, :],
+                    start=True,
+                    stop=True,
                 )
-                shift = work.tile([P, PAIR], F32, bufs=HALVES * GROUPS)
-                nc.scalar.mul(out=shift[:], in_=top[:], mul=-SCALE)
-                for e in range(PAIR):
-                    t = PAIR * u + e
-                    nc.scalar.activation(
-                        out=expd[:, t, :],
-                        in_=aff_banks[i, u][:, e, :],
-                        func=mybir.ActivationFunctionType.Exp,
-                        bias=shift[:, e : e + 1],
-                        scale=SCALE,
-                        accum_out=total[:, t : t + 1],
-                    )
-            inverse = work.tile([P, PACK], F32)
-            nc.vector.reciprocal(out=inverse[:], in_=total[:])
-            exps[i] = (expd, inverse)
 
-        def normalise(i):
-            expd, inverse = exps[i]
-            grouped = work.tile([P, Q, PACK], BF16, align_bytes=64)
-            engine = nc.gpsimd if i == 0 else nc.vector
+        def maxima(b, es):
+            if b not in tops:
+                tops[b] = work.tile([P, PAIR], F32, bufs=HALVES * GROUPS, name="top")
+            source = aff_banks[b][:, es, :] if b > 0 else aff_tiles[b, es.start]
+            nc.vector.tensor_reduce(out=tops[b][:, es], in_=source, axis=mybir.AxisListType.X, op=mybir.AluOpType.max)
+
+        def bias(b, es):
+            if b not in shifts:
+                shifts[b] = work.tile([P, PAIR], F32, bufs=HALVES * GROUPS, name="shift")
+            nc.scalar.mul(out=shifts[b][:, es], in_=tops[b][:, es], mul=-SCALE)
+
+        def exponentials(b, e):
+            i, u = divmod(b, HALVES)
+            if i not in exps:
+                expd = work.tile([P, PACK, Q], F32)
+                total = work.tile([P, PACK], F32)
+                inverse = work.tile([P, PACK], F32)
+                exps[i] = (expd, total, inverse)
+            expd, total, inverse = exps[i]
+            t = PAIR * u + e
+            nc.scalar.activation(
+                out=expd[:, t, :],
+                in_=aff_tiles[b, e].rearrange("p e q -> p (e q)"),
+                func=mybir.ActivationFunctionType.Exp,
+                bias=shifts[b][:, e : e + 1],
+                scale=SCALE,
+                accum_out=total[:, t : t + 1],
+            )
+
+        def invert(i, ts):
+            expd, total, inverse = exps[i]
+            nc.vector.reciprocal(out=inverse[:, ts], in_=total[:, ts])
+
+        def normalise(engine, i, ts, qs):
+            expd, total, inverse = exps[i]
+            shape = [P, qs.stop - qs.start, ts.stop - ts.start]
             engine.tensor_tensor(
-                out=grouped[:],
-                in0=expd[:].rearrange("p t q -> p q t"),
-                in1=inverse[:].unsqueeze(1).to_broadcast([P, Q, PACK]),
+                out=attn_grouped[:, i, qs, ts],
+                in0=expd[:, ts, qs].rearrange("p t q -> p q t"),
+                in1=inverse[:, ts].unsqueeze(1).to_broadcast(shape),
                 op=mybir.AluOpType.mult,
             )
-            attn_grouped[i] = grouped
 
-        def transpose_values(n):
-            turned = work.tile([P, PASSES, CV, PACK], BF16, align_bytes=64)
-            for g in range(PASSES):
-                landing = psum.tile([P, HALVES, C_TILES, P], F32, tag="bank")
-                for u in range(HALVES):
-                    for j in range(C_TILES):
-                        words = mv_sb[:, n, j, :].bitcast(F32)
-                        first = (K_PASS * g + PAIR * P * u) // PAIR
-                        nc.tensor.transpose(landing[:, u, j, :], words[:, first : first + P], ident[:])
-                nc.scalar.copy(
-                    out=turned[:, g].rearrange("p c t -> p (c t)").bitcast(F32).rearrange("p (c u) -> p c u", u=HALVES),
-                    in_=landing[:].rearrange("p u j r -> p (j r) u"),
-                )
-            mv_grouped[n] = turned
+        def transpose_values(i):
+            n, g = divmod(i, PASSES)
+            landing = psum.tile([P, HALVES, C_TILES, P], F32, tag="bank")
+            for u in range(HALVES):
+                for j in range(C_TILES):
+                    words = mv_sb[:, n, j, :].bitcast(F32)
+                    first = (K_PASS * g + PAIR * P * u) // PAIR
+                    nc.tensor.transpose(landing[:, u, j, :], words[:, first : first + P], ident[:])
+            landings[i] = landing
+
+        def group_values(i):
+            nc.scalar.copy(
+                out=mv_grouped[:, i].rearrange("p c t -> p (c t)").bitcast(F32).rearrange("p (c u) -> p c u", u=HALVES),
+                in_=landings[i][:].rearrange("p u j r -> p (j r) u"),
+            )
 
         def quantise_values(n):
             both = slice(PASSES * n, PASSES * (n + 1))
             nc.vector.quantize_mx(
                 out=mv_codes[:, both, :].rearrange("p g c -> p (g c)").bitcast(FP8X4),
                 scales=mv_scales[:, both, :].rearrange("p g c -> p (g c)"),
-                in_=mv_grouped[n][:].rearrange("p g c t -> p (g c t)"),
+                in_=mv_grouped[:, both].rearrange("p g c t -> p (g c t)"),
             )
 
-        def quantise_attn(i):
+        def quantise_attn(groups, qs):
             nc.vector.quantize_mx(
-                out=attn_codes[:, i, :].bitcast(FP8X4),
-                scales=attn_scales[:, i, :],
-                in_=attn_grouped[i][:].rearrange("p q t -> p (q t)"),
+                out=attn_codes[:, groups, qs].rearrange("p g q -> p (g q)").bitcast(FP8X4),
+                scales=attn_scales[:, groups, qs].rearrange("p g q -> p (g q)"),
+                in_=attn_grouped[:, groups, qs].rearrange("p g q t -> p (g q t)"),
             )
 
-        def read_out(i):
+        def read_out(i, j, qs):
             n, g = divmod(i, PASSES)
-            for j in range(C_TILES):
-                if g == 0:
-                    sums[n, j] = psum.tile([P, Q], F32, tag="bank", name="mapped_sum")
-                channels = slice(P * j, P * (j + 1))
-                nc.tensor.matmul_mx(
-                    out=sums[n, j][:],
-                    lhsT=mv_codes[:, i, channels].bitcast(FP8X4),
-                    lhsT_scale=mv_scales[:, i, channels],
-                    rhs=attn_codes[:, i, :].bitcast(FP8X4),
-                    rhs_scale=attn_scales[:, i, :],
-                    start=(g == 0),
-                    stop=(g == PASSES - 1),
-                )
-            if g == PASSES - 1:
-                for j in range(C_TILES):
-                    mapped = work.tile([P, Q], F32)
-                    nc.scalar.copy(out=mapped[:], in_=sums[n, j][:])
-                    rows = slice(CV + P * j, CV + P * (j + 1))
-                    nc.sync.dma_start(out=out[n, rows].rearrange("r h w -> r (h w)"), in_=mapped[:])
+            if (n, j, qs.start) not in sums:
+                sums[n, j, qs.start] = psum.tile([P, qs.stop - qs.start], F32, tag="bank", name="mapped_sum")
+            channels = slice(P * j, P * (j + 1))
+            nc.tensor.matmul_mx(
+                out=sums[n, j, qs.start][:],
+                lhsT=mv_codes[:, i, channels].bitcast(FP8X4),
+                lhsT_scale=mv_scales[:, i, channels],
+                rhs=attn_codes[:, i, qs].bitcast(FP8X4),
+                rhs_scale=attn_scales[:, i, qs],
+                start=(g == 0),
+                stop=(g == PASSES - 1),
+            )
+
+        def store_mapped(n, j, qs, copy):
+            mapped = work.tile([P, qs.stop - qs.start], F32, bufs=6)
+            copy(out=mapped[:], in_=sums[n, j, qs.start][:])
+            rows = slice(CV + P * j, CV + P * (j + 1))
+            nc.sync.dma_start(out=out[n, rows].rearrange("r h w -> r (h w)")[:, qs], in_=mapped[:])
 
         def pass_query_values():
+            wide = keep.tile([P, SAMPLES, C_TILES, Q], F32)
+            nc.gpsimd.tensor_scalar(
+                out=wide[:],
+                in0=qv_sb[:],
+                scalar1=1.0,
+                scalar2=0.0,
+                op0=mybir.AluOpType.mult,
+                op1=mybir.AluOpType.add,
+            )
             for n in range(SAMPLES):
-                wide = work.tile([P, C_TILES, Q], F32)
-                nc.gpsimd.tensor_scalar(
-                    out=wide[:],
-                    in0=qv_sb[:, n],
-                    scalar1=1.0,
-                    scalar2=0.0,
-                    op0=mybir.AluOpType.mult,
-                    op1=mybir.AluOpType.add,
-                )
-                nc.sync.dma_start(out=out[n, 0:CV].rearrange("(j r) h w -> r j (h w)", r=P), in_=wide[:])
+                nc.sync.dma_start(out=out[n, 0:CV].rearrange("(j r) h w -> r j (h w)", r=P), in_=wide[:, n])
 
-        for i in range(GROUPS):
-            affinity(i)
-        pass_query_values()
-        for i in range(GROUPS + 3):
-            if i < GROUPS:
-                exponentials(i)
-            if 1 <= i <= SAMPLES:
-                transpose_values(i - 1)
-            if 0 <= i - 2 < GROUPS:
-                normalise(i - 2)
-            if 0 <= i - 3 < GROUPS:
-                if i - 3 < SAMPLES:
-                    quantise_values(i - 3)
-                quantise_attn(i - 3)
-                read_out(i - 3)
+        everything = slice(0, PACK)
+        both = slice(0, PAIR)
+        all_q = slice(0, Q)
+        q_halves = (slice(0, Q // 2), slice(Q // 2, Q))
+        with tc.manual_schedule():
+            for b in range(HALVES * GROUPS):
+                affinity(b)
+            pass_query_values()
+            for e in range(PAIR):
+                maxima(0, slice(e, e + 1))
+                bias(0, slice(e, e + 1))
+                exponentials(0, e)
+            maxima(1, both)
+            bias(1, both)
+            for b in range(1, HALVES * GROUPS):
+                if b + 1 < HALVES * GROUPS:
+                    maxima(b + 1, both)
+                exponentials(b, 0)
+                if b + 1 < HALVES * GROUPS:
+                    bias(b + 1, both)
+                exponentials(b, 1)
+                if b == 1:
+                    invert(0, slice(0, 2))
+                    normalise(nc.gpsimd, 0, slice(0, 2), all_q)
+                if b == 3:
+                    invert(0, slice(2, 4))
+                    normalise(nc.gpsimd, 0, slice(2, 4), all_q)
+            for i in range(GROUPS):
+                transpose_values(i)
+                group_values(i)
+            invert(1, everything)
+            normalise(nc.vector, 1, everything, all_q)
+            invert(2, everything)
+            normalise(nc.vector, 2, everything, all_q)
+            quantise_attn(slice(0, 2), all_q)
+            invert(3, everything)
+            quantise_attn(slice(2, 3), all_q)
+            normalise(nc.vector, 3, everything, q_halves[0])
+            quantise_values(0)
+            for i in range(PASSES):
+                for j in range(C_TILES):
+                    read_out(i, j, all_q)
+            for j in range(C_TILES):
+                store_mapped(0, j, all_q, nc.scalar.copy)
+            normalise(nc.vector, 3, everything, q_halves[1])
+            quantise_values(1)
+            for qs in q_halves:
+                quantise_attn(slice(3, 4), qs)
+            for qs in q_halves:
+                for i in range(PASSES, GROUPS):
+                    for j in range(C_TILES):
+                        read_out(i, j, qs)
+                store_mapped(1, 0, qs, nc.scalar.copy)
+                store_mapped(1, 1, qs, nc.vector.tensor_copy)

@@ -46,8 +46,8 @@ def tile_stm_head_s_kernel(tc, q_key, q_val, m_key, m_val, out):
             nc.sync.dma_start(out=mk_sb[:, n, columns], in_=m_key[n].rearrange("c t h w -> c (t h w)")[:, columns])
 
         load_queries(0)
-        load_keys(0, slice(0, K_PASS))
-        load_keys(0, slice(K_PASS, M))
+        load_keys(0, slice(0, K_PASS // HALVES))
+        load_keys(0, slice(K_PASS // HALVES, M))
         nc.sync.dma_start(
             out=qv_sb[:].rearrange("r n j q -> r (n j) q"), in_=q_val.rearrange("n (j r) h w -> r (n j) (h w)", r=P)
         )
@@ -225,6 +225,8 @@ def tile_stm_head_s_kernel(tc, q_key, q_val, m_key, m_val, out):
                 if b + 1 < HALVES * GROUPS:
                     bias(b + 1, both)
                 exponentials(b, 1)
+                if b == 5:
+                    invert(1, everything)
                 if b == 1:
                     invert(0, slice(0, 2))
                     normalise(nc.gpsimd, 0, slice(0, 2), all_q)
@@ -234,24 +236,24 @@ def tile_stm_head_s_kernel(tc, q_key, q_val, m_key, m_val, out):
             for i in range(GROUPS):
                 transpose_values(i)
                 group_values(i)
-            invert(1, everything)
             normalise(nc.vector, 1, everything, all_q)
             invert(2, everything)
+            quantise_attn(slice(0, 1), all_q)
             normalise(nc.vector, 2, everything, all_q)
-            quantise_attn(slice(0, 2), all_q)
             invert(3, everything)
-            quantise_attn(slice(2, 3), all_q)
+            quantise_attn(slice(1, 2), all_q)
             normalise(nc.vector, 3, everything, q_halves[0])
+            normalise(nc.vector, 3, everything, q_halves[1])
+            quantise_attn(slice(2, 3), all_q)
             quantise_values(0)
             for i in range(PASSES):
                 for j in range(C_TILES):
                     read_out(i, j, all_q)
-            for j in range(C_TILES):
-                store_mapped(0, j, all_q, nc.scalar.copy)
-            normalise(nc.vector, 3, everything, q_halves[1])
             quantise_values(1)
             for qs in q_halves:
                 quantise_attn(slice(3, 4), qs)
+            store_mapped(0, 0, all_q, nc.scalar.copy)
+            store_mapped(0, 1, all_q, nc.vector.tensor_copy)
             for qs in q_halves:
                 for i in range(PASSES, GROUPS):
                     for j in range(C_TILES):

@@ -23,6 +23,7 @@ HALVES = 2
 PAIR = 2
 C_TILES = CV // P
 SCALE = 1.0 / math.sqrt(CK)
+RUN = 4
 
 FLOPS = 2 * SAMPLES * Q * M * (CK + CV)
 
@@ -131,11 +132,12 @@ def tile_stm_head_s_kernel(tc, q_key, q_val, m_key, m_val, out):
 
         def normalise(engine, i, ts, qs):
             expd, total, inverse = exps[i]
-            shape = [P, qs.stop - qs.start, ts.stop - ts.start]
+            runs = (qs.stop - qs.start) // RUN
+            shape = [P, runs, ts.stop - ts.start, RUN]
             engine.tensor_tensor(
-                out=attn_grouped[:, i, qs, ts],
-                in0=expd[:, ts, qs].rearrange("p t q -> p q t"),
-                in1=inverse[:, ts].unsqueeze(1).to_broadcast(shape),
+                out=attn_grouped[:, i, qs, ts].rearrange("p (c r) t -> p c t r", r=RUN),
+                in0=expd[:, ts, qs].rearrange("p t (c r) -> p c t r", r=RUN),
+                in1=inverse[:, ts].unsqueeze(1).unsqueeze(3).to_broadcast(shape),
                 op=mybir.AluOpType.mult,
             )
 

@@ -23,6 +23,7 @@ HALVES = 2
 PAIR = 2
 C_TILES = CV // P
 SCALE = 1.0 / math.sqrt(CK)
+SINGLES = 2
 RUN = 4
 
 FLOPS = 2 * SAMPLES * Q * M * (CK + CV)
@@ -40,19 +41,19 @@ def tile_stm_head_s_kernel(tc, q_key, q_val, m_key, m_val, out):
         mv_sb = keep.tile([P, SAMPLES, C_TILES, M], BF16)
         qv_sb = keep.tile([P, SAMPLES, C_TILES, Q], BF16)
 
-        def load_queries(n):
-            nc.sync.dma_start(out=qk_sb[:, n, :], in_=q_key[n].rearrange("c h w -> c (h w)"))
+        def load_queries(n, engine):
+            engine.dma_start(out=qk_sb[:, n, :], in_=q_key[n].rearrange("c h w -> c (h w)"))
 
         def load_keys(n, columns):
             nc.sync.dma_start(out=mk_sb[:, n, columns], in_=m_key[n].rearrange("c t h w -> c (t h w)")[:, columns])
 
-        load_queries(0)
+        load_queries(0, nc.scalar)
         load_keys(0, slice(0, K_PASS // HALVES))
         load_keys(0, slice(K_PASS // HALVES, M))
         nc.sync.dma_start(
             out=qv_sb[:].rearrange("r n j q -> r (n j) q"), in_=q_val.rearrange("n (j r) h w -> r (n j) (h w)", r=P)
         )
-        load_queries(1)
+        load_queries(1, nc.sync)
         load_keys(1, slice(0, M))
         for n in range(SAMPLES):
             nc.sync.dma_start(out=mv_sb[:, n], in_=m_val[n].rearrange("(j r) t h w -> r j (t h w)", r=P))
@@ -81,7 +82,7 @@ def tile_stm_head_s_kernel(tc, q_key, q_val, m_key, m_val, out):
         def affinity(b):
             n, g, u = b // (PASSES * HALVES), b // HALVES % PASSES, b % HALVES
             keys = mk_sb[:, n, :].rearrange("c (g u p e) -> c g u e p", g=PASSES, u=HALVES, e=PAIR)
-            if b == 0:
+            if b < SINGLES:
                 tiles = [psum.tile([P, 1, Q], F32, tag="bank", name="first_bank")[:] for e in range(PAIR)]
             else:
                 bank = psum.tile([P, PAIR, Q], F32, tag="bank")
@@ -100,7 +101,7 @@ def tile_stm_head_s_kernel(tc, q_key, q_val, m_key, m_val, out):
         def maxima(b, es):
             if b not in tops:
                 tops[b] = work.tile([P, PAIR], F32, bufs=HALVES * GROUPS, name="top")
-            source = aff_banks[b][:, es, :] if b > 0 else aff_tiles[b, es.start]
+            source = aff_banks[b][:, es, :] if b >= SINGLES else aff_tiles[b, es.start]
             nc.vector.tensor_reduce(out=tops[b][:, es], in_=source, axis=mybir.AxisListType.X, op=mybir.AluOpType.max)
 
         def bias(b, es):
@@ -157,12 +158,11 @@ def tile_stm_head_s_kernel(tc, q_key, q_val, m_key, m_val, out):
                 in_=landings[i][:].rearrange("p u j r -> p (j r) u"),
             )
 
-        def quantise_values(n):
-            both = slice(PASSES * n, PASSES * (n + 1))
+        def quantise_values(groups):
             nc.vector.quantize_mx(
-                out=mv_codes[:, both, :].rearrange("p g c -> p (g c)").bitcast(FP8X4),
-                scales=mv_scales[:, both, :].rearrange("p g c -> p (g c)"),
-                in_=mv_grouped[:, both].rearrange("p g c t -> p (g c t)"),
+                out=mv_codes[:, groups, :].rearrange("p g c -> p (g c)").bitcast(FP8X4),
+                scales=mv_scales[:, groups, :].rearrange("p g c -> p (g c)"),
+                in_=mv_grouped[:, groups].rearrange("p g c t -> p (g c t)"),
             )
 
         def quantise_attn(groups, qs):
@@ -214,12 +214,13 @@ def tile_stm_head_s_kernel(tc, q_key, q_val, m_key, m_val, out):
             for b in range(HALVES * GROUPS):
                 affinity(b)
             pass_query_values()
-            for e in range(PAIR):
-                maxima(0, slice(e, e + 1))
-                bias(0, slice(e, e + 1))
-                exponentials(0, e)
-            maxima(1, both)
-            bias(1, both)
+            tiles = [(b, e) for b in range(SINGLES) for e in range(PAIR)]
+            ahead = 2
+            for k, (b, e) in enumerate(tiles):
+                maxima(b, slice(e, e + 1))
+                bias(b, slice(e, e + 1))
+                if k + 1 >= ahead and k + 1 - ahead < PAIR:
+                    exponentials(*tiles[k + 1 - ahead])
             for b in range(1, HALVES * GROUPS):
                 if b + 1 < HALVES * GROUPS:
                     maxima(b + 1, both)
@@ -245,20 +246,23 @@ def tile_stm_head_s_kernel(tc, q_key, q_val, m_key, m_val, out):
             invert(3, everything)
             quantise_attn(slice(1, 2), all_q)
             normalise(nc.vector, 3, everything, q_halves[0])
-            normalise(nc.vector, 3, everything, q_halves[1])
-            quantise_attn(slice(2, 3), all_q)
-            quantise_values(0)
+            quantise_values(slice(0, PASSES))
             for i in range(PASSES):
                 for j in range(C_TILES):
                     read_out(i, j, all_q)
-            quantise_values(1)
+            for j in range(C_TILES):
+                store_mapped(0, j, all_q, nc.scalar.copy)
+            normalise(nc.vector, 3, everything, q_halves[1])
+            quantise_attn(slice(2, 3), all_q)
+            quantise_values(slice(2, 3))
+            for qs in q_halves:
+                for j in range(C_TILES):
+                    read_out(PASSES, j, qs)
+            quantise_values(slice(3, 4))
             for qs in q_halves:
                 quantise_attn(slice(3, 4), qs)
-            store_mapped(0, 0, all_q, nc.scalar.copy)
-            store_mapped(0, 1, all_q, nc.vector.tensor_copy)
             for qs in q_halves:
-                for i in range(PASSES, GROUPS):
-                    for j in range(C_TILES):
-                        read_out(i, j, qs)
+                for j in range(C_TILES):
+                    read_out(PASSES + 1, j, qs)
                 store_mapped(1, 0, qs, nc.scalar.copy)
                 store_mapped(1, 1, qs, nc.vector.tensor_copy)

@@ -23,6 +23,7 @@ HALVES = 2
 PAIR = 2
 C_TILES = CV // P
 SCALE = 1.0 / math.sqrt(CK)
+WARM_UPS = 4
 SINGLES = 2
 RUN = 4
 
@@ -158,6 +159,14 @@ def tile_stm_head_s_kernel(tc, q_key, q_val, m_key, m_val, out):
                 in_=landings[i][:].rearrange("p u j r -> p (j r) u"),
             )
 
+        def warm_tensor_engine(i):
+            expd, total, inverse = exps[i]
+            bank = psum.tile([P, WARM_UPS, P], F32, tag="bank")
+            for w in range(WARM_UPS):
+                nc.tensor.matmul(
+                    out=bank[:, w, :], lhsT=expd[:, 0, 0:P], rhs=expd[:, 1, 0:P], start=True, stop=True
+                )
+
         def quantise_values(groups):
             nc.vector.quantize_mx(
                 out=mv_codes[:, groups, :].rearrange("p g c -> p (g c)").bitcast(FP8X4),
@@ -239,6 +248,7 @@ def tile_stm_head_s_kernel(tc, q_key, q_val, m_key, m_val, out):
             for i in range(GROUPS):
                 transpose_values(i)
                 group_values(i)
+            warm_tensor_engine(GROUPS - 1)
             normalise(nc.vector, 1, everything, all_q)
             invert(2, everything)
             quantise_attn(slice(0, 1), all_q)

@@ -134,11 +134,12 @@ def tile_stm_head_s_kernel(tc, q_key, q_val, m_key, m_val, out):
 
         def normalise(engine, i, ts, qs):
             expd, total, inverse = exps[i]
-            runs = (qs.stop - qs.start) // RUN
-            shape = [P, runs, ts.stop - ts.start, RUN]
+            run = 1 if i == 0 else RUN
+            runs = (qs.stop - qs.start) // run
+            shape = [P, runs, ts.stop - ts.start, run]
             engine.tensor_tensor(
-                out=attn_grouped[:, i, qs, ts].rearrange("p (c r) t -> p c t r", r=RUN),
-                in0=expd[:, ts, qs].rearrange("p t (c r) -> p c t r", r=RUN),
+                out=attn_grouped[:, i, qs, ts].rearrange("p (c r) t -> p c t r", r=run),
+                in0=expd[:, ts, qs].rearrange("p t (c r) -> p c t r", r=run),
                 in1=inverse[:, ts].unsqueeze(1).unsqueeze(3).to_broadcast(shape),
                 op=mybir.AluOpType.mult,
             )
@@ -196,11 +197,11 @@ def tile_stm_head_s_kernel(tc, q_key, q_val, m_key, m_val, out):
                 stop=(g == PASSES - 1),
             )
 
-        def store_mapped(n, j, qs, copy):
+        def store_mapped(n, j, qs, copy, queue=nc.sync):
             mapped = work.tile([P, qs.stop - qs.start], F32, bufs=6)
             copy(out=mapped[:], in_=sums[n, j, qs.start][:])
             rows = slice(CV + P * j, CV + P * (j + 1))
-            nc.sync.dma_start(out=out[n, rows].rearrange("r h w -> r (h w)")[:, qs], in_=mapped[:])
+            queue.dma_start(out=out[n, rows].rearrange("r h w -> r (h w)")[:, qs], in_=mapped[:])
 
         def pass_query_values():
             wide = keep.tile([P, SAMPLES, C_TILES, Q], F32)
@@ -274,5 +275,5 @@ def tile_stm_head_s_kernel(tc, q_key, q_val, m_key, m_val, out):
             for qs in q_halves:
                 for j in range(C_TILES):
                     read_out(PASSES + 1, j, qs)
-                store_mapped(1, 0, qs, nc.scalar.copy)
+                store_mapped(1, 0, qs, nc.scalar.copy, nc.scalar if qs is q_halves[-1] else nc.sync)
                 store_mapped(1, 1, qs, nc.vector.tensor_copy)

@@ -77,6 +77,7 @@ def tile_stm_head_s_kernel(tc, q_key, q_val, m_key, m_val, out):
         tops = {}
         shifts = {}
         exps = {}
+        scaled_on_scalar = {}
         landings = {}
         sums = {}
 
@@ -142,6 +143,24 @@ def tile_stm_head_s_kernel(tc, q_key, q_val, m_key, m_val, out):
                 in0=expd[:, ts, qs].rearrange("p t (c r) -> p c t r", r=run),
                 in1=inverse[:, ts].unsqueeze(1).unsqueeze(3).to_broadcast(shape),
                 op=mybir.AluOpType.mult,
+            )
+
+        def scale_on_scalar(i, qs):
+            expd, total, inverse = exps[i]
+            scaled = keep.tile([P, PACK, qs.stop - qs.start], BF16)
+            for t in range(PACK):
+                nc.scalar.activation(
+                    out=scaled[:, t, :],
+                    in_=expd[:, t, qs],
+                    func=mybir.ActivationFunctionType.Copy,
+                    scale=inverse[:, t : t + 1],
+                )
+            scaled_on_scalar[i] = scaled
+
+        def interleave(i, qs):
+            nc.vector.tensor_copy(
+                out=attn_grouped[:, i, qs, :].rearrange("p (c r) t -> p c t r", r=RUN),
+                in_=scaled_on_scalar[i][:].rearrange("p t (c r) -> p c t r", r=RUN),
             )
 
         def transpose_values(i):
@@ -261,15 +280,16 @@ def tile_stm_head_s_kernel(tc, q_key, q_val, m_key, m_val, out):
             for i in range(PASSES):
                 for j in range(C_TILES):
                     read_out(i, j, all_q)
+            scale_on_scalar(3, q_halves[1])
+            quantise_attn(slice(2, 3), all_q)
             for j in range(C_TILES):
                 store_mapped(0, j, all_q, nc.scalar.copy)
-            normalise(nc.vector, 3, everything, q_halves[1])
-            quantise_attn(slice(2, 3), all_q)
             quantise_values(slice(2, 3))
             for qs in q_halves:
                 for j in range(C_TILES):
                     read_out(PASSES, j, qs)
             quantise_values(slice(3, 4))
+            interleave(3, q_halves[1])
             for qs in q_halves:
                 quantise_attn(slice(3, 4), qs)
             for qs in q_halves:

import math

import concourse.mybir as mybir
from concourse.masks import make_identity

F32 = mybir.dt.float32
BF16 = mybir.dt.bfloat16
U32 = mybir.dt.uint32
U8 = mybir.dt.uint8
FP8X4 = mybir.dt.float8_e4m3fn_x4

P = 128
SAMPLES = 2
CK = 128
CV = 256
Q = 256
M = 1024
PACK = 4
K_PASS = P * PACK
PASSES = M // K_PASS
GROUPS = SAMPLES * PASSES
HALVES = 2
PAIR = 2
C_TILES = CV // P
SCALE = 1.0 / math.sqrt(CK)
WARM_UPS = 4
SINGLES = 2
RUN = 4

FLOPS = 2 * SAMPLES * Q * M * (CK + CV)


def tile_stm_head_s_kernel(tc, q_key, q_val, m_key, m_val, out):
    nc = tc.nc
    with (
        tc.tile_pool(name="keep", bufs=1) as keep,
        tc.tile_pool(name="work", bufs=GROUPS) as work,
        tc.psum_pool(name="psum", bufs=8) as psum,
    ):
        qk_sb = keep.tile([P, SAMPLES, Q], BF16)
        mk_sb = keep.tile([P, SAMPLES, M], BF16)
        mv_sb = keep.tile([P, SAMPLES, C_TILES, M], BF16)
        qv_sb = keep.tile([P, SAMPLES, C_TILES, Q], BF16)

        def load_queries(n, engine):
            engine.dma_start(out=qk_sb[:, n, :], in_=q_key[n].rearrange("c h w -> c (h w)"))

        def load_keys(n, columns):
            nc.sync.dma_start(out=mk_sb[:, n, columns], in_=m_key[n].rearrange("c t h w -> c (t h w)")[:, columns])

        load_queries(0, nc.scalar)
        load_keys(0, slice(0, K_PASS // HALVES))
        load_keys(0, slice(K_PASS // HALVES, M))
        nc.sync.dma_start(
            out=qv_sb[:].rearrange("r n j q -> r (n j) q"), in_=q_val.rearrange("n (j r) h w -> r (n j) (h w)", r=P)
        )
        load_queries(1, nc.sync)
        load_keys(1, slice(0, M))
        for n in range(SAMPLES):
            nc.sync.dma_start(out=mv_sb[:, n], in_=m_val[n].rearrange("(j r) t h w -> r j (t h w)", r=P))

        ident = keep.tile([P, P], F32)
        make_identity(nc, ident[:])
        warm = keep.tile([P, 1], F32)
        nc.vector.memset(warm[:], 0.0)
        nc.scalar.activation(out=warm[:], in_=warm[:], func=mybir.ActivationFunctionType.Exp)

        attn_codes = keep.tile([P, GROUPS, Q], U32, align_bytes=64)
        attn_scales = keep.tile([P, GROUPS, Q], U8, align_bytes=64)
        mv_codes = keep.tile([P, GROUPS, CV], U32, align_bytes=64)
        mv_scales = keep.tile([P, GROUPS, CV], U8, align_bytes=64)
        attn_grouped = keep.tile([P, GROUPS, Q, PACK], BF16, align_bytes=64)
        mv_grouped = keep.tile([P, GROUPS, CV, PACK], BF16, align_bytes=64)

        aff_banks = {}
        aff_tiles = {}
        tops = {}
        shifts = {}
        exps = {}
        scaled_on_scalar = {}
        landings = {}
        sums = {}

        def affinity(b):
            n, g, u = b // (PASSES * HALVES), b // HALVES % PASSES, b % HALVES
            keys = mk_sb[:, n, :].rearrange("c (g u p e) -> c g u e p", g=PASSES, u=HALVES, e=PAIR)
            if b < SINGLES:
                tiles = [psum.tile([P, 1, Q], F32, tag="bank", name="first_bank")[:] for e in range(PAIR)]
            else:
                bank = psum.tile([P, PAIR, Q], F32, tag="bank")
                tiles = [bank[:, e : e + 1, :] for e in range(PAIR)]
                aff_banks[b] = bank
            for e in range(PAIR):
                aff_tiles[b, e] = tiles[e]
                nc.tensor.matmul(
                    out=tiles[e].rearrange("p e q -> p (e q)"),
                    lhsT=keys[:, g, u, e, :],
                    rhs=qk_sb[:, n, :],
                    start=True,
                    stop=True,
                )

        def maxima(b, es):
            if b not in tops:
                tops[b] = work.tile([P, PAIR], F32, bufs=HALVES * GROUPS, name="top")
            source = aff_banks[b][:, es, :] if b >= SINGLES else aff_tiles[b, es.start]
            nc.vector.tensor_reduce(out=tops[b][:, es], in_=source, axis=mybir.AxisListType.X, op=mybir.AluOpType.max)

        def bias(b, es):
            if b not in shifts:
                shifts[b] = work.tile([P, PAIR], F32, bufs=HALVES * GROUPS, name="shift")
            nc.scalar.mul(out=shifts[b][:, es], in_=tops[b][:, es], mul=-SCALE)

        def exponentials(b, e):
            i, u = divmod(b, HALVES)
            if i not in exps:
                expd = work.tile([P, PACK, Q], F32)
                total = work.tile([P, PACK], F32)
                inverse = work.tile([P, PACK], F32)
                exps[i] = (expd, total, inverse)
            expd, total, inverse = exps[i]
            t = PAIR * u + e
            nc.scalar.activation(
                out=expd[:, t, :],
                in_=aff_tiles[b, e].rearrange("p e q -> p (e q)"),
                func=mybir.ActivationFunctionType.Exp,
                bias=shifts[b][:, e : e + 1],
                scale=SCALE,
                accum_out=total[:, t : t + 1],
            )

        def invert(i, ts):
            expd, total, inverse = exps[i]
            nc.vector.reciprocal(out=inverse[:, ts], in_=total[:, ts])

        def normalise(engine, i, ts, qs):
            expd, total, inverse = exps[i]
            run = 1 if i == 0 else RUN
            runs = (qs.stop - qs.start) // run
            shape = [P, runs, ts.stop - ts.start, run]
            engine.tensor_tensor(
                out=attn_grouped[:, i, qs, ts].rearrange("p (c r) t -> p c t r", r=run),
                in0=expd[:, ts, qs].rearrange("p t (c r) -> p c t r", r=run),
                in1=inverse[:, ts].unsqueeze(1).unsqueeze(3).to_broadcast(shape),
                op=mybir.AluOpType.mult,
            )

        def scale_on_scalar(i, qs):
            expd, total, inverse = exps[i]
            scaled = keep.tile([P, PACK, qs.stop - qs.start], BF16)
            for t in range(PACK):
                nc.scalar.activation(
                    out=scaled[:, t, :],
                    in_=expd[:, t, qs],
                    func=mybir.ActivationFunctionType.Copy,
                    scale=inverse[:, t : t + 1],
                )
            scaled_on_scalar[i] = scaled

        def interleave(i, qs):
            nc.vector.tensor_copy(
                out=attn_grouped[:, i, qs, :].rearrange("p (c r) t -> p c t r", r=RUN),
                in_=scaled_on_scalar[i][:].rearrange("p t (c r) -> p c t r", r=RUN),
            )

        def transpose_values(i):
            n, g = divmod(i, PASSES)
            landing = psum.tile([P, HALVES, C_TILES, P], F32, tag="bank")
            for u in range(HALVES):
                for j in range(C_TILES):
                    words = mv_sb[:, n, j, :].bitcast(F32)
                    first = (K_PASS * g + PAIR * P * u) // PAIR
                    nc.tensor.transpose(landing[:, u, j, :], words[:, first : first + P], ident[:])
            landings[i] = landing

        def group_values(i):
            nc.scalar.copy(
                out=mv_grouped[:, i].rearrange("p c t -> p (c t)").bitcast(F32).rearrange("p (c u) -> p c u", u=HALVES),
                in_=landings[i][:].rearrange("p u j r -> p (j r) u"),
            )

        def warm_tensor_engine(i):
            expd, total, inverse = exps[i]
            bank = psum.tile([P, WARM_UPS, P], F32, tag="bank")
            for w in range(WARM_UPS):
                nc.tensor.matmul(
                    out=bank[:, w, :], lhsT=expd[:, 0, 0:P], rhs=expd[:, 1, 0:P], start=True, stop=True
                )

        def quantise_values(groups):
            nc.vector.quantize_mx(
                out=mv_codes[:, groups, :].rearrange("p g c -> p (g c)").bitcast(FP8X4),
                scales=mv_scales[:, groups, :].rearrange("p g c -> p (g c)"),
                in_=mv_grouped[:, groups].rearrange("p g c t -> p (g c t)"),
            )

        def quantise_attn(groups, qs):
            nc.vector.quantize_mx(
                out=attn_codes[:, groups, qs].rearrange("p g q -> p (g q)").bitcast(FP8X4),
                scales=attn_scales[:, groups, qs].rearrange("p g q -> p (g q)"),
                in_=attn_grouped[:, groups, qs].rearrange("p g q t -> p (g q t)"),
            )

        def read_out(i, j, qs):
            n, g = divmod(i, PASSES)
            if (n, j, qs.start) not in sums:
                sums[n, j, qs.start] = psum.tile([P, qs.stop - qs.start], F32, tag="bank", name="mapped_sum")
            channels = slice(P * j, P * (j + 1))
            nc.tensor.matmul_mx(
                out=sums[n, j, qs.start][:],
                lhsT=mv_codes[:, i, channels].bitcast(FP8X4),
                lhsT_scale=mv_scales[:, i, channels],
                rhs=attn_codes[:, i, qs].bitcast(FP8X4),
                rhs_scale=attn_scales[:, i, qs],
                start=(g == 0),
                stop=(g == PASSES - 1),
            )

        def store_mapped(n, j, qs, copy, queue=nc.sync):
            mapped = work.tile([P, qs.stop - qs.start], F32, bufs=6)
            copy(out=mapped[:], in_=sums[n, j, qs.start][:])
            rows = slice(CV + P * j, CV + P * (j + 1))
            queue.dma_start(out=out[n, rows].rearrange("r h w -> r (h w)")[:, qs], in_=mapped[:])

        def pass_query_values():
            wide = keep.tile([P, SAMPLES, C_TILES, Q], F32)
            nc.gpsimd.tensor_scalar(
                out=wide[:],
                in0=qv_sb[:],
                scalar1=1.0,
                scalar2=0.0,
                op0=mybir.AluOpType.mult,
                op1=mybir.AluOpType.add,
            )
            for n in range(SAMPLES):
                nc.sync.dma_start(out=out[n, 0:CV].rearrange("(j r) h w -> r j (h w)", r=P), in_=wide[:, n])

        everything = slice(0, PACK)
        both = slice(0, PAIR)
        all_q = slice(0, Q)
        q_halves = (slice(0, Q // 2), slice(Q // 2, Q))
        with tc.manual_schedule():
            for b in range(HALVES * GROUPS):
                affinity(b)
            pass_query_values()
            tiles = [(b, e) for b in range(SINGLES) for e in range(PAIR)]
            ahead = 2
            for k, (b, e) in enumerate(tiles):
                maxima(b, slice(e, e + 1))
                bias(b, slice(e, e + 1))
                if k + 1 >= ahead and k + 1 - ahead < PAIR:
                    exponentials(*tiles[k + 1 - ahead])
            for b in range(1, HALVES * GROUPS):
                if b + 1 < HALVES * GROUPS:
                    maxima(b + 1, both)
                exponentials(b, 0)
                if b + 1 < HALVES * GROUPS:
                    bias(b + 1, both)
                exponentials(b, 1)
                if b == 5:
                    invert(1, everything)
                if b == 1:
                    invert(0, slice(0, 2))
                    normalise(nc.gpsimd, 0, slice(0, 2), all_q)
                if b == 3:
                    invert(0, slice(2, 4))
                    normalise(nc.gpsimd, 0, slice(2, 4), all_q)
            for i in range(GROUPS):
                transpose_values(i)
                group_values(i)
            warm_tensor_engine(GROUPS - 1)
            normalise(nc.vector, 1, everything, all_q)
            invert(2, everything)
            quantise_attn(slice(0, 1), all_q)
            normalise(nc.vector, 2, everything, all_q)
            invert(3, everything)
            quantise_attn(slice(1, 2), all_q)
            normalise(nc.vector, 3, everything, q_halves[0])
            quantise_values(slice(0, PASSES))
            for i in range(PASSES):
                for j in range(C_TILES):
                    read_out(i, j, all_q)
            scale_on_scalar(3, q_halves[1])
            quantise_attn(slice(2, 3), all_q)
            for j in range(C_TILES):
                store_mapped(0, j, all_q, nc.scalar.copy)
            quantise_values(slice(2, 3))
            for qs in q_halves:
                for j in range(C_TILES):
                    read_out(PASSES, j, qs)
            quantise_values(slice(3, 4))
            interleave(3, q_halves[1])
            for qs in q_halves:
                quantise_attn(slice(3, 4), qs)
            for qs in q_halves:
                for j in range(C_TILES):
                    read_out(PASSES + 1, j, qs)
                store_mapped(1, 0, qs, nc.scalar.copy, nc.scalar if qs is q_halves[-1] else nc.sync)
                store_mapped(1, 1, qs, nc.vector.tensor_copy)
